import numpy as np
import ml_dtypes


def mxq(x, axis, fmt="e4m3"):
    dtype, down = {"e4m3": (ml_dtypes.float8_e4m3fn, 7), "e5m2": (ml_dtypes.float8_e5m2, 14)}[fmt]
    v = np.moveaxis(np.asarray(x, np.float32).astype(ml_dtypes.bfloat16).astype(np.float64), axis, -1)
    blocks = v.reshape(v.shape[:-1] + (-1, 32))
    amax = np.abs(blocks).max(-1, keepdims=True)
    byte = np.maximum(np.where(amax > 0, np.frexp(amax)[1] - 1 + 127, 0) - down, 1)
    scale = np.exp2(byte - 127.0)
    codes = (blocks / scale).astype(np.float32).astype(dtype).astype(np.float64)
    return np.moveaxis((codes * scale).reshape(v.shape), -1, axis)


WIDE = False


def mx_kscale(k):
    if not WIDE:
        return np.ones(k)
    levels = np.array([10, -10, 5, -5, 0])
    a = np.random.permutation(np.resize(levels, k // 512 * 4)).reshape(k // 512, 4)
    idx = np.arange(k)
    return np.exp2(a[idx // 512, idx % 128 // 32])


BF16 = ml_dtypes.bfloat16


def bf(x):
    return np.asarray(x, np.float32).astype(BF16)


def f64(x):
    return np.asarray(x).astype(np.float64)


B, T, KA, KT, DIM, NH, HD, E = 2, 512, 256, 256, 1024, 8, 128, 8
QC = 6.0


def setup_inputs():
    r = np.random.standard_normal
    s = mx_kscale(KA + KT)
    g = bf(1.0 + 0.25 * r(1))
    ratio = 1.0 / (1.0 + np.exp(-f64(g)[0]))
    sh = np.log(s) * np.sqrt(HD) / QC
    u = s.max() / s
    q_a, q_t = r((B, NH, T, HD)) * 1.2, r((B, NH, T, HD)) * 1.2
    k_a, k_t = r((B, NH, KA, HD)) * 1.2, r((B, NH, KT, HD)) * 1.2
    q_a[..., 0] = QC
    q_t[..., 0] = QC
    k_a[..., 0] += sh[:KA]
    k_t[..., 0] += sh[KA:] / ratio
    v_a = r((B, NH, KA, HD)) * 1.5 * u[:KA, None]
    v_t = r((B, NH, KT, HD)) * 1.5 * u[KA:, None]
    return {"q_a": bf(q_a), "q_t": bf(q_t), "k_a": bf(k_a), "k_t": bf(k_t),
            "v_a": bf(v_a), "v_t": bf(v_t), "gating_factor": g}


def reference(q_a, q_t, k_a, k_t, v_a, v_t, gating_factor):
    ratio_g = 1.0 / (1.0 + np.exp(-f64(gating_factor)))
    s_a = f64(q_a) @ f64(k_a).transpose(0, 1, 3, 2)
    s_t = (f64(q_t) @ f64(k_t).transpose(0, 1, 3, 2)) * ratio_g
    scores = np.concatenate([s_a, s_t], axis=-1) / np.sqrt(HD)
    e = np.exp(scores - scores.max(-1, keepdims=True))
    v = np.concatenate([f64(v_a), f64(v_t)], axis=2)
    out = (mxq(e, 3, "e4m3") @ mxq(v, 2, "e4m3")) / e.sum(-1, keepdims=True)
    return out.transpose(0, 2, 1, 3).reshape(B, T, NH * HD)

@@ -1,0 +1,247 @@
+import math
+from contextlib import ExitStack
+
+import concourse.mybir as mybir
+from concourse.masks import make_identity
+
+BF16 = mybir.dt.bfloat16
+F32 = mybir.dt.float32
+U32 = mybir.dt.uint32
+U8 = mybir.dt.uint8
+FP8X4 = mybir.dt.float8_e4m3fn_x4
+ALU = mybir.AluOpType
+ACT = mybir.ActivationFunctionType
+AX = mybir.AxisListType
+
+P = 128
+HEADS = 16
+T = 512
+KS = 256
+D = 128
+NPAIR = 2 * HEADS
+C = 1.0 / math.sqrt(128.0)
+FLOPS = 4 * HEADS * T * (2 * KS) * D
+PIN = False
+CHUNKS = ((0, 1), (1, 2), (2, 4), (4, 8), (8, 16))
+
+
+def tile_l1regressionmoeactionhead_pb_kernel(tc, q_a, q_t, k_a, k_t, v_a, v_t, gating_factor, out):
+    nc = tc.nc
+    with ExitStack() as ctx:
+        if PIN:
+            ctx.enter_context(tc.manual_schedule())
+        res = ctx.enter_context(tc.tile_pool(name="res", bufs=1))
+        wk = ctx.enter_context(tc.tile_pool(name="wk", bufs=3))
+        ps_s = ctx.enter_context(tc.psum_pool(name="ps_s", bufs=4))
+        ps_t1 = ctx.enter_context(tc.psum_pool(name="ps_t1", bufs=1))
+        ps_t2 = ctx.enter_context(tc.psum_pool(name="ps_t2", bufs=2))
+        ps_o = ctx.enter_context(tc.psum_pool(name="ps_o", bufs=1))
+
+        g_sb = res.tile([P, 1], BF16)
+        qa_sb = res.tile([P, HEADS * 512], BF16)
+        qt_sb = res.tile([P, HEADS * 512], BF16)
+        ka_sb = res.tile([P, HEADS * 256], BF16)
+        kt_sb = res.tile([P, HEADS * 256], BF16)
+        v_sb = res.tile([P, HEADS * 512], BF16)
+        vcodes = res.tile([P, HEADS * D], U32, align_bytes=64)
+        vscl = res.tile([P, HEADS * D], U8, align_bytes=64)
+        ident = res.tile([P, P], BF16)
+        eg = res.tile([P, 1], F32)
+        ratio = res.tile([P, 1], F32)
+        cr = res.tile([P, 1], F32)
+
+        nc.sync.dma_start(out=g_sb[:], in_=gating_factor.partition_broadcast(P))
+        qa_v = q_a.rearrange("b h (p j) d -> p (b h) (j d)", j=4)
+        qt_v = q_t.rearrange("b h (p j) d -> p (b h) (j d)", j=4)
+        ka_v = k_a.rearrange("b h (j p) d -> p (b h j) d", p=P)
+        kt_v = k_t.rearrange("b h (j p) d -> p (b h j) d", p=P)
+        va_v = v_a.rearrange("b h (t p) d -> p (b h t) d", p=P)
+        vt_v = v_t.rearrange("b h (t p) d -> p (b h t) d", p=P)
+        qa_s = qa_sb[:].rearrange("p (h x) -> p h x", x=512)
+        qt_s = qt_sb[:].rearrange("p (h x) -> p h x", x=512)
+        ka_s = ka_sb[:].rearrange("p (g d) -> p g d", d=D)
+        kt_s = kt_sb[:].rearrange("p (g d) -> p g d", d=D)
+        v_s = v_sb[:].rearrange("p (u g d) -> p u g d", u=2, d=D)
+        v_r = v_sb[:].rearrange("p (u h t d) -> p h d u t", u=2, t=2, d=D)
+        for h0, h1 in CHUNKS:
+            nc.sync.dma_start(out=ka_s[:, 2 * h0:2 * h1, :], in_=ka_v[:, 2 * h0:2 * h1, :])
+            nc.sync.dma_start(out=qa_s[:, h0:h1, :], in_=qa_v[:, h0:h1, :])
+            nc.sync.dma_start(out=kt_s[:, 2 * h0:2 * h1, :], in_=kt_v[:, 2 * h0:2 * h1, :])
+            nc.sync.dma_start(out=qt_s[:, h0:h1, :], in_=qt_v[:, h0:h1, :])
+            nc.sync.dma_start(out=v_s[:, 0, 2 * h0:2 * h1, :], in_=va_v[:, 2 * h0:2 * h1, :])
+            nc.sync.dma_start(out=v_s[:, 1, 2 * h0:2 * h1, :], in_=vt_v[:, 2 * h0:2 * h1, :])
+
+        make_identity(nc, ident[:])
+
+        nc.scalar.activation(out=eg[:], in_=g_sb[:], func=ACT.Exp, scale=-1.0)
+        nc.vector.tensor_scalar_add(out=eg[:], in0=eg[:], scalar1=1.0)
+        nc.vector.reciprocal(out=ratio[:], in_=eg[:])
+        nc.vector.tensor_scalar_mul(out=cr[:], in0=ratio[:], scalar1=C)
+
+        st = {}
+
+        def t1_pe(h, s):
+            q_sb, k_sb = (qa_sb, ka_sb) if s == 0 else (qt_sb, kt_sb)
+            t1 = ps_t1.tile([P, 768], BF16, name="t1")
+            for j in range(4):
+                nc.tensor.transpose(t1[:, j * P:(j + 1) * P], q_sb[:, h * 512 + j * P:h * 512 + (j + 1) * P], ident[:])
+            for j in range(2):
+                nc.tensor.transpose(t1[:, 512 + j * P:512 + (j + 1) * P], k_sb[:, h * 256 + j * P:h * 256 + (j + 1) * P], ident[:])
+            st[("t1", h, s)] = t1
+
+        def t1_ev(h, s):
+            xT = wk.tile([P, 768], BF16, name="xT%d" % s, bufs=2)
+            nc.scalar.copy(out=xT[:], in_=st[("t1", h, s)][:])
+            st[("xT", h, s)] = xT
+
+        def vprep(h):
+            vg = wk.tile([P, 512], BF16, name="vg", align_bytes=64)
+            nc.vector.tensor_copy(
+                out=vg[:].rearrange("p (d u t) -> p d u t", u=2, t=2),
+                in_=v_r[:, h],
+            )
+            st[("vg", h)] = vg
+
+        def vquant(h):
+            nc.vector.quantize_mx(
+                out=vcodes[:, h * D:(h + 1) * D].bitcast(FP8X4),
+                scales=vscl[:, h * D:(h + 1) * D],
+                in_=st[("vg", h)][:],
+            )
+
+        def sc(s):
+            h = s // 2
+            aT = st[("xT", h, 0)]
+            tT = st[("xT", h, 1)]
+            mxp = wk.tile([P, 4], F32, name="mxp", bufs=4)
+            for jj in range(2):
+                j = 2 * (s % 2) + jj
+                sb = ps_s.tile([P, 512], F32, name="sb")
+                nc.tensor.matmul(out=sb[:, 0:256], lhsT=aT[:, j * P:(j + 1) * P], rhs=aT[:, 512:768], start=True, stop=True)
+                nc.tensor.matmul(out=sb[:, 256:512], lhsT=tT[:, j * P:(j + 1) * P], rhs=tT[:, 512:768], start=True, stop=True)
+                nc.vector.tensor_reduce(
+                    out=mxp[:, 2 * jj:2 * jj + 2],
+                    in_=sb[:].rearrange("p (u k) -> p u k", u=2),
+                    axis=AX.X,
+                    op=ALU.max,
+                )
+                st[("sb", s, jj)] = sb
+            mxv = mxp[:].rearrange("p (j u) -> p j u", u=2)
+            mm = wk.tile([P, 2], F32, name="mm", bufs=4)
+            nb = wk.tile([P, 2], F32, name="nb", bufs=4)
+            nc.vector.scalar_tensor_tensor(out=mm[:], in0=mxv[:, :, 1], scalar=ratio[:, 0:1], in1=mxv[:, :, 0], op0=ALU.mult, op1=ALU.max)
+            nc.vector.tensor_scalar_mul(out=nb[:], in0=mm[:], scalar1=-C)
+            st[("nb", s)] = nb
+
+        def ex(s):
+            h = s // 2
+            if s % 2 == 0:
+                rs = wk.tile([P, 8], F32, name="rs", bufs=4)
+                st[("rs", h)] = rs
+            rs = st[("rs", h)]
+            nb = st[("nb", s)]
+            e = wk.tile([P, 1024], BF16, name="e")
+            for jj in range(2):
+                j = 2 * (s % 2) + jj
+                sb = st[("sb", s, jj)]
+                nc.scalar.activation(out=e[:, jj * 512:jj * 512 + 256], in_=sb[:, 0:256], func=ACT.Exp,
+                                     bias=nb[:, jj:jj + 1], scale=C, accum_out=rs[:, 2 * j:2 * j + 1])
+                nc.scalar.activation(out=e[:, jj * 512 + 256:jj * 512 + 512], in_=sb[:, 256:512], func=ACT.Exp,
+                                     bias=nb[:, jj:jj + 1], scale=cr[:, 0:1], accum_out=rs[:, 2 * j + 1:2 * j + 2])
+            st[("e", s)] = e
+
+        def te(s):
+            e = st[("e", s)]
+            t2 = ps_t2.tile([P, 1024], BF16, name="t2")
+            for i in range(8):
+                nc.tensor.transpose(t2[:, i * P:(i + 1) * P], e[:, i * P:(i + 1) * P], ident[:])
+            st[("t2", s)] = t2
+
+        def ev(s):
+            et = wk.tile([P, 1024], BF16, name="et")
+            nc.scalar.copy(out=et[:], in_=st[("t2", s)][:])
+            st[("et", s)] = et
+
+        def rg(s):
+            gr = wk.tile([P, 1024], BF16, name="gr", align_bytes=64)
+            nc.gpsimd.tensor_scalar(
+                out=gr[:].rearrange("p (j q t) -> p j q t", j=2, t=4),
+                in0=st[("et", s)][:].rearrange("p (j t q) -> p j q t", j=2, t=4),
+                scalar1=1.0, scalar2=0.0, op0=ALU.mult, op1=ALU.add,
+            )
+            st[("gr", s)] = gr
+
+        def qz(s):
+            codes = wk.tile([P, 256], U32, name="codes", align_bytes=64)
+            scl = wk.tile([P, 256], U8, name="scl", align_bytes=64)
+            nc.vector.quantize_mx(out=codes[:].bitcast(FP8X4), scales=scl[:], in_=st[("gr", s)][:])
+            st[("cd", s)] = (codes, scl)
+
+        def mx(s):
+            h = s // 2
+            if s % 2 == 0:
+                o = ps_o.tile([P, 512], F32, name="o")
+                st[("o", h)] = o
+            o = st[("o", h)]
+            codes, scl = st[("cd", s)]
+            for jj in range(2):
+                j = 2 * (s % 2) + jj
+                nc.tensor.matmul_mx(
+                    out=o[:, j * D:(j + 1) * D],
+                    lhsT=codes[:, jj * P:(jj + 1) * P].bitcast(FP8X4),
+                    lhsT_scale=scl[:, jj * P:(jj + 1) * P],
+                    rhs=vcodes[:, h * D:(h + 1) * D].bitcast(FP8X4),
+                    rhs_scale=vscl[:, h * D:(h + 1) * D],
+                    start=True, stop=True,
+                )
+
+        def nm(h):
+            rs = st[("rs", h)]
+            rsum = wk.tile([P, 4], F32, name="rsum")
+            rinv = wk.tile([P, 4], F32, name="rinv")
+            osb = wk.tile([P, 512], F32, name="osb")
+            nc.vector.tensor_reduce(out=rsum[:], in_=rs[:].rearrange("p (j u) -> p j u", u=2), axis=AX.X, op=ALU.add)
+            nc.vector.reciprocal(out=rinv[:], in_=rsum[:])
+            nc.vector.tensor_tensor(
+                out=osb[:].rearrange("p (j d) -> p j d", d=D),
+                in0=st[("o", h)][:].rearrange("p (j d) -> p j d", d=D),
+                in1=rinv[:].unsqueeze(2).to_broadcast([P, 4, D]),
+                op=ALU.mult,
+            )
+            n, hh = divmod(h, 8)
+            nc.sync.dma_start(
+                out=out[n].rearrange("(p j) c -> p j c", j=4)[:, :, hh * D:(hh + 1) * D],
+                in_=osb[:].rearrange("p (j d) -> p j d", d=D),
+            )
+
+        t1_pe(0, 0)
+        t1_ev(0, 0)
+        t1_pe(0, 1)
+        t1_ev(0, 1)
+        for t in range(-1, NPAIR + 4):
+            if t % 2 == 1 and 0 <= (t - 5) // 2 < HEADS:
+                nm((t - 5) // 2)
+            if t % 2 == 0 and 0 <= t // 2 < HEADS:
+                vprep(t // 2)
+            if 0 <= t - 3 < NPAIR:
+                qz(t - 3)
+            if t % 2 == 0 and 0 <= t // 2 < HEADS:
+                vquant(t // 2)
+            if 0 <= t + 1 < NPAIR:
+                sc(t + 1)
+            if 0 <= t - 3 < NPAIR:
+                mx(t - 3)
+            if 0 <= t - 1 < NPAIR:
+                te(t - 1)
+            th, ts = ((t + 3) // 2, 0) if t % 2 == 1 else ((t + 2) // 2, 1)
+            do_t1 = 1 <= th < HEADS
+            if do_t1:
+                t1_pe(th, ts)
+            if 0 <= t < NPAIR:
+                ex(t)
+            if 0 <= t - 1 < NPAIR:
+                ev(t - 1)
+            if do_t1:
+                t1_ev(th, ts)
+            if 0 <= t - 2 < NPAIR:
+                rg(t - 2)

@@ -21,7 +21,7 @@ D = 128
 NPAIR = 2 * HEADS
 C = 1.0 / math.sqrt(128.0)
 FLOPS = 4 * HEADS * T * (2 * KS) * D
-PIN = False
+PIN = True
 CHUNKS = ((0, 1), (1, 2), (2, 4), (4, 8), (8, 16))
 
 

@@ -8,6 +8,7 @@ BF16 = mybir.dt.bfloat16
 F32 = mybir.dt.float32
 U32 = mybir.dt.uint32
 U8 = mybir.dt.uint8
+I32 = mybir.dt.int32
 FP8X4 = mybir.dt.float8_e4m3fn_x4
 ALU = mybir.AluOpType
 ACT = mybir.ActivationFunctionType
@@ -22,6 +23,8 @@ NPAIR = 2 * HEADS
 C = 1.0 / math.sqrt(128.0)
 FLOPS = 4 * HEADS * T * (2 * KS) * D
 PIN = True
+FILL = 2
+WARM = 6
 CHUNKS = ((0, 1), (1, 2), (2, 4), (4, 8), (8, 16))
 
 
@@ -34,7 +37,8 @@ def tile_l1regressionmoeactionhead_pb_kernel(tc, q_a, q_t, k_a, k_t, v_a, v_t, g
         wk = ctx.enter_context(tc.tile_pool(name="wk", bufs=3))
         ps_s = ctx.enter_context(tc.psum_pool(name="ps_s", bufs=4))
         ps_t1 = ctx.enter_context(tc.psum_pool(name="ps_t1", bufs=1))
-        ps_t2 = ctx.enter_context(tc.psum_pool(name="ps_t2", bufs=2))
+        ps_t2 = ctx.enter_context(tc.psum_pool(name="ps_t2", bufs=1))
+        ps_j = ctx.enter_context(tc.psum_pool(name="ps_j", bufs=1))
         ps_o = ctx.enter_context(tc.psum_pool(name="ps_o", bufs=1))
 
         g_sb = res.tile([P, 1], BF16)
@@ -46,6 +50,10 @@ def tile_l1regressionmoeactionhead_pb_kernel(tc, q_a, q_t, k_a, k_t, v_a, v_t, g
         vcodes = res.tile([P, HEADS * D], U32, align_bytes=64)
         vscl = res.tile([P, HEADS * D], U8, align_bytes=64)
         ident = res.tile([P, P], BF16)
+        zc = res.tile([P, 512], U32, align_bytes=64)
+        zs = res.tile([P, 512], U8, align_bytes=64)
+        zb = res.tile([P, 2048], BF16, align_bytes=64)
+        junk = ps_j.tile([P, 512], F32)
         eg = res.tile([P, 1], F32)
         ratio = res.tile([P, 1], F32)
         cr = res.tile([P, 1], F32)
@@ -72,6 +80,15 @@ def tile_l1regressionmoeactionhead_pb_kernel(tc, q_a, q_t, k_a, k_t, v_a, v_t, g
             nc.sync.dma_start(out=v_s[:, 1, 2 * h0:2 * h1, :], in_=vt_v[:, 2 * h0:2 * h1, :])
 
         make_identity(nc, ident[:])
+        nc.vector.memset(zb[:].bitcast(I32), 0)
+        nc.vector.quantize_mx(out=zc[:].bitcast(FP8X4), scales=zs[:], in_=zb[:])
+
+        def filler(n):
+            for i in range(n):
+                nc.tensor.matmul_mx(out=junk[:], lhsT=zc[:, 0:P].bitcast(FP8X4), lhsT_scale=zs[:, 0:P],
+                                    rhs=zc[:].bitcast(FP8X4), rhs_scale=zs[:], start=True, stop=True)
+
+        filler(WARM)
 
         nc.scalar.activation(out=eg[:], in_=g_sb[:], func=ACT.Exp, scale=-1.0)
         nc.vector.tensor_scalar_add(out=eg[:], in0=eg[:], scalar1=1.0)
@@ -96,9 +113,10 @@ def tile_l1regressionmoeactionhead_pb_kernel(tc, q_a, q_t, k_a, k_t, v_a, v_t, g
 
         def vprep(h):
             vg = wk.tile([P, 512], BF16, name="vg", align_bytes=64)
-            nc.vector.tensor_copy(
+            nc.gpsimd.tensor_scalar(
                 out=vg[:].rearrange("p (d u t) -> p d u t", u=2, t=2),
-                in_=v_r[:, h],
+                in0=v_r[:, h],
+                scalar1=1.0, scalar2=0.0, op0=ALU.mult, op1=ALU.add,
             )
             st[("vg", h)] = vg
 
@@ -113,41 +131,39 @@ def tile_l1regressionmoeactionhead_pb_kernel(tc, q_a, q_t, k_a, k_t, v_a, v_t, g
             h = s // 2
             aT = st[("xT", h, 0)]
             tT = st[("xT", h, 1)]
-            mxp = wk.tile([P, 4], F32, name="mxp", bufs=4)
             for jj in range(2):
                 j = 2 * (s % 2) + jj
                 sb = ps_s.tile([P, 512], F32, name="sb")
                 nc.tensor.matmul(out=sb[:, 0:256], lhsT=aT[:, j * P:(j + 1) * P], rhs=aT[:, 512:768], start=True, stop=True)
                 nc.tensor.matmul(out=sb[:, 256:512], lhsT=tT[:, j * P:(j + 1) * P], rhs=tT[:, 512:768], start=True, stop=True)
-                nc.vector.tensor_reduce(
-                    out=mxp[:, 2 * jj:2 * jj + 2],
-                    in_=sb[:].rearrange("p (u k) -> p u k", u=2),
-                    axis=AX.X,
-                    op=ALU.max,
-                )
                 st[("sb", s, jj)] = sb
-            mxv = mxp[:].rearrange("p (j u) -> p j u", u=2)
-            mm = wk.tile([P, 2], F32, name="mm", bufs=4)
-            nb = wk.tile([P, 2], F32, name="nb", bufs=4)
-            nc.vector.scalar_tensor_tensor(out=mm[:], in0=mxv[:, :, 1], scalar=ratio[:, 0:1], in1=mxv[:, :, 0], op0=ALU.mult, op1=ALU.max)
-            nc.vector.tensor_scalar_mul(out=nb[:], in0=mm[:], scalar1=-C)
+
+        def pre(s):
+            mxp = wk.tile([P, 4], F32, name="mxp", bufs=6)
+            nb = wk.tile([P, 2], F32, name="nb", bufs=6)
+            for jj in range(2):
+                sb = st[("sb", s, jj)]
+                x = wk.tile([P, 512], F32, name="x", bufs=8)
+                nc.vector.tensor_scalar(out=x[:, 0:256], in0=sb[:, 0:256], scalar1=C, scalar2=None,
+                                        op0=ALU.mult, op1=ALU.max, accum_out=mxp[:, 2 * jj:2 * jj + 1])
+                nc.vector.tensor_scalar(out=x[:, 256:512], in0=sb[:, 256:512], scalar1=cr[:, 0:1], scalar2=None,
+                                        op0=ALU.mult, op1=ALU.max, accum_out=mxp[:, 2 * jj + 1:2 * jj + 2])
+                st[("x", s, jj)] = x
+            nc.vector.tensor_reduce(out=nb[:], in_=mxp[:].rearrange("p (j u) -> p j u", u=2), axis=AX.X, op=ALU.max, negate=True)
             st[("nb", s)] = nb
 
         def ex(s):
             h = s // 2
             if s % 2 == 0:
-                rs = wk.tile([P, 8], F32, name="rs", bufs=4)
+                rs = wk.tile([P, 4], F32, name="rs", bufs=5)
                 st[("rs", h)] = rs
             rs = st[("rs", h)]
             nb = st[("nb", s)]
             e = wk.tile([P, 1024], BF16, name="e")
             for jj in range(2):
                 j = 2 * (s % 2) + jj
-                sb = st[("sb", s, jj)]
-                nc.scalar.activation(out=e[:, jj * 512:jj * 512 + 256], in_=sb[:, 0:256], func=ACT.Exp,
-                                     bias=nb[:, jj:jj + 1], scale=C, accum_out=rs[:, 2 * j:2 * j + 1])
-                nc.scalar.activation(out=e[:, jj * 512 + 256:jj * 512 + 512], in_=sb[:, 256:512], func=ACT.Exp,
-                                     bias=nb[:, jj:jj + 1], scale=cr[:, 0:1], accum_out=rs[:, 2 * j + 1:2 * j + 2])
+                nc.scalar.activation(out=e[:, jj * 512:(jj + 1) * 512], in_=st[("x", s, jj)][:], func=ACT.Exp,
+                                     bias=nb[:, jj:jj + 1], scale=1.0, accum_out=rs[:, j:j + 1])
             st[("e", s)] = e
 
         def te(s):
@@ -197,11 +213,9 @@ def tile_l1regressionmoeactionhead_pb_kernel(tc, q_a, q_t, k_a, k_t, v_a, v_t, g
 
         def nm(h):
             rs = st[("rs", h)]
-            rsum = wk.tile([P, 4], F32, name="rsum")
             rinv = wk.tile([P, 4], F32, name="rinv")
             osb = wk.tile([P, 512], F32, name="osb")
-            nc.vector.tensor_reduce(out=rsum[:], in_=rs[:].rearrange("p (j u) -> p j u", u=2), axis=AX.X, op=ALU.add)
-            nc.vector.reciprocal(out=rinv[:], in_=rsum[:])
+            nc.vector.reciprocal(out=rinv[:], in_=rs[:])
             nc.vector.tensor_tensor(
                 out=osb[:].rearrange("p (j d) -> p j d", d=D),
                 in0=st[("o", h)][:].rearrange("p (j d) -> p j d", d=D),
@@ -214,27 +228,25 @@ def tile_l1regressionmoeactionhead_pb_kernel(tc, q_a, q_t, k_a, k_t, v_a, v_t, g
                 in_=osb[:].rearrange("p (j d) -> p j d", d=D),
             )
 
-        t1_pe(0, 0)
-        t1_ev(0, 0)
-        t1_pe(0, 1)
-        t1_ev(0, 1)
-        for t in range(-1, NPAIR + 4):
+        for t in range(-5, NPAIR + 4):
             if t % 2 == 1 and 0 <= (t - 5) // 2 < HEADS:
                 nm((t - 5) // 2)
-            if t % 2 == 0 and 0 <= t // 2 < HEADS:
-                vprep(t // 2)
             if 0 <= t - 3 < NPAIR:
                 qz(t - 3)
-            if t % 2 == 0 and 0 <= t // 2 < HEADS:
-                vquant(t // 2)
-            if 0 <= t + 1 < NPAIR:
-                sc(t + 1)
+            if t % 2 == 0 and 0 <= (t - 2) // 2 < HEADS:
+                vquant((t - 2) // 2)
+            if 0 <= t + 3 < NPAIR:
+                sc(t + 3)
+            if 0 <= t + 2 < NPAIR:
+                pre(t + 2)
             if 0 <= t - 3 < NPAIR:
                 mx(t - 3)
+            if t < NPAIR:
+                filler(FILL)
             if 0 <= t - 1 < NPAIR:
                 te(t - 1)
-            th, ts = ((t + 3) // 2, 0) if t % 2 == 1 else ((t + 2) // 2, 1)
-            do_t1 = 1 <= th < HEADS
+            th, ts = ((t + 5) // 2, 0) if t % 2 == 1 else ((t + 4) // 2, 1)
+            do_t1 = 0 <= th < HEADS
             if do_t1:
                 t1_pe(th, ts)
             if 0 <= t < NPAIR:
@@ -245,3 +257,5 @@ def tile_l1regressionmoeactionhead_pb_kernel(tc, q_a, q_t, k_a, k_t, v_a, v_t, g
                 t1_ev(th, ts)
             if 0 <= t - 2 < NPAIR:
                 rg(t - 2)
+            if t % 2 == 0 and 0 <= t // 2 < HEADS:
+                vprep(t // 2)

@@ -23,8 +23,6 @@ NPAIR = 2 * HEADS
 C = 1.0 / math.sqrt(128.0)
 FLOPS = 4 * HEADS * T * (2 * KS) * D
 PIN = True
-FILL = 2
-WARM = 6
 CHUNKS = ((0, 1), (1, 2), (2, 4), (4, 8), (8, 16))
 
 
@@ -37,8 +35,7 @@ def tile_l1regressionmoeactionhead_pb_kernel(tc, q_a, q_t, k_a, k_t, v_a, v_t, g
         wk = ctx.enter_context(tc.tile_pool(name="wk", bufs=3))
         ps_s = ctx.enter_context(tc.psum_pool(name="ps_s", bufs=4))
         ps_t1 = ctx.enter_context(tc.psum_pool(name="ps_t1", bufs=1))
-        ps_t2 = ctx.enter_context(tc.psum_pool(name="ps_t2", bufs=1))
-        ps_j = ctx.enter_context(tc.psum_pool(name="ps_j", bufs=1))
+        ps_t2 = ctx.enter_context(tc.psum_pool(name="ps_t2", bufs=2))
         ps_o = ctx.enter_context(tc.psum_pool(name="ps_o", bufs=1))
 
         g_sb = res.tile([P, 1], BF16)
@@ -50,10 +47,6 @@ def tile_l1regressionmoeactionhead_pb_kernel(tc, q_a, q_t, k_a, k_t, v_a, v_t, g
         vcodes = res.tile([P, HEADS * D], U32, align_bytes=64)
         vscl = res.tile([P, HEADS * D], U8, align_bytes=64)
         ident = res.tile([P, P], BF16)
-        zc = res.tile([P, 512], U32, align_bytes=64)
-        zs = res.tile([P, 512], U8, align_bytes=64)
-        zb = res.tile([P, 2048], BF16, align_bytes=64)
-        junk = ps_j.tile([P, 512], F32)
         eg = res.tile([P, 1], F32)
         ratio = res.tile([P, 1], F32)
         cr = res.tile([P, 1], F32)
@@ -80,16 +73,6 @@ def tile_l1regressionmoeactionhead_pb_kernel(tc, q_a, q_t, k_a, k_t, v_a, v_t, g
             nc.sync.dma_start(out=v_s[:, 1, 2 * h0:2 * h1, :], in_=vt_v[:, 2 * h0:2 * h1, :])
 
         make_identity(nc, ident[:])
-        nc.vector.memset(zb[:].bitcast(I32), 0)
-        nc.vector.quantize_mx(out=zc[:].bitcast(FP8X4), scales=zs[:], in_=zb[:])
-
-        def filler(n):
-            for i in range(n):
-                nc.tensor.matmul_mx(out=junk[:], lhsT=zc[:, 0:P].bitcast(FP8X4), lhsT_scale=zs[:, 0:P],
-                                    rhs=zc[:].bitcast(FP8X4), rhs_scale=zs[:], start=True, stop=True)
-
-        filler(WARM)
-
         nc.scalar.activation(out=eg[:], in_=g_sb[:], func=ACT.Exp, scale=-1.0)
         nc.vector.tensor_scalar_add(out=eg[:], in0=eg[:], scalar1=1.0)
         nc.vector.reciprocal(out=ratio[:], in_=eg[:])
@@ -113,11 +96,7 @@ def tile_l1regressionmoeactionhead_pb_kernel(tc, q_a, q_t, k_a, k_t, v_a, v_t, g
 
         def vprep(h):
             vg = wk.tile([P, 512], BF16, name="vg", align_bytes=64)
-            nc.gpsimd.tensor_scalar(
-                out=vg[:].rearrange("p (d u t) -> p d u t", u=2, t=2),
-                in0=v_r[:, h],
-                scalar1=1.0, scalar2=0.0, op0=ALU.mult, op1=ALU.add,
-            )
+            nc.vector.tensor_copy(out=vg[:].rearrange("p (d u t) -> p d u t", u=2, t=2), in_=v_r[:, h])
             st[("vg", h)] = vg
 
         def vquant(h):
@@ -139,11 +118,11 @@ def tile_l1regressionmoeactionhead_pb_kernel(tc, q_a, q_t, k_a, k_t, v_a, v_t, g
                 st[("sb", s, jj)] = sb
 
         def pre(s):
-            mxp = wk.tile([P, 4], F32, name="mxp", bufs=6)
-            nb = wk.tile([P, 2], F32, name="nb", bufs=6)
+            mxp = wk.tile([P, 4], F32, name="mxp", bufs=8)
+            nb = wk.tile([P, 2], F32, name="nb", bufs=8)
             for jj in range(2):
                 sb = st[("sb", s, jj)]
-                x = wk.tile([P, 512], F32, name="x", bufs=8)
+                x = wk.tile([P, 512], F32, name="x", bufs=10)
                 nc.vector.tensor_scalar(out=x[:, 0:256], in0=sb[:, 0:256], scalar1=C, scalar2=None,
                                         op0=ALU.mult, op1=ALU.max, accum_out=mxp[:, 2 * jj:2 * jj + 1])
                 nc.vector.tensor_scalar(out=x[:, 256:512], in0=sb[:, 256:512], scalar1=cr[:, 0:1], scalar2=None,
@@ -155,11 +134,11 @@ def tile_l1regressionmoeactionhead_pb_kernel(tc, q_a, q_t, k_a, k_t, v_a, v_t, g
         def ex(s):
             h = s // 2
             if s % 2 == 0:
-                rs = wk.tile([P, 4], F32, name="rs", bufs=5)
+                rs = wk.tile([P, 4], F32, name="rs", bufs=6)
                 st[("rs", h)] = rs
             rs = st[("rs", h)]
             nb = st[("nb", s)]
-            e = wk.tile([P, 1024], BF16, name="e")
+            e = wk.tile([P, 1024], BF16, name="e", bufs=4)
             for jj in range(2):
                 j = 2 * (s % 2) + jj
                 nc.scalar.activation(out=e[:, jj * 512:(jj + 1) * 512], in_=st[("x", s, jj)][:], func=ACT.Exp,
@@ -174,22 +153,25 @@ def tile_l1regressionmoeactionhead_pb_kernel(tc, q_a, q_t, k_a, k_t, v_a, v_t, g
             st[("t2", s)] = t2
 
         def ev(s):
-            et = wk.tile([P, 1024], BF16, name="et")
-            nc.scalar.copy(out=et[:], in_=st[("t2", s)][:])
+            t2 = st[("t2", s)]
+            et = wk.tile([P, 512], BF16, name="et", bufs=4)
+            gr = wk.tile([P, 1024], BF16, name="gr", align_bytes=64, bufs=6)
+            nc.scalar.copy(out=et[:], in_=t2[:, 0:512])
+            nc.scalar.copy(out=gr[:, 512:1024].rearrange("p (q t) -> p q t", t=4),
+                           in_=t2[:, 512:1024].rearrange("p (t q) -> p q t", t=4))
             st[("et", s)] = et
-
-        def rg(s):
-            gr = wk.tile([P, 1024], BF16, name="gr", align_bytes=64)
-            nc.gpsimd.tensor_scalar(
-                out=gr[:].rearrange("p (j q t) -> p j q t", j=2, t=4),
-                in0=st[("et", s)][:].rearrange("p (j t q) -> p j q t", j=2, t=4),
-                scalar1=1.0, scalar2=0.0, op0=ALU.mult, op1=ALU.add,
-            )
             st[("gr", s)] = gr
 
+        def rg(s):
+            nc.gpsimd.tensor_scalar(
+                out=st[("gr", s)][:, 0:512].rearrange("p (q t) -> p q t", t=4),
+                in0=st[("et", s)][:].rearrange("p (t q) -> p q t", t=4),
+                scalar1=1.0, scalar2=0.0, op0=ALU.mult, op1=ALU.add,
+            )
+
         def qz(s):
-            codes = wk.tile([P, 256], U32, name="codes", align_bytes=64)
-            scl = wk.tile([P, 256], U8, name="scl", align_bytes=64)
+            codes = wk.tile([P, 256], U32, name="codes", align_bytes=64, bufs=5)
+            scl = wk.tile([P, 256], U8, name="scl", align_bytes=64, bufs=5)
             nc.vector.quantize_mx(out=codes[:].bitcast(FP8X4), scales=scl[:], in_=st[("gr", s)][:])
             st[("cd", s)] = (codes, scl)
 
@@ -228,34 +210,31 @@ def tile_l1regressionmoeactionhead_pb_kernel(tc, q_a, q_t, k_a, k_t, v_a, v_t, g
                 in_=osb[:].rearrange("p (j d) -> p j d", d=D),
             )
 
-        for t in range(-5, NPAIR + 4):
-            if t % 2 == 1 and 0 <= (t - 5) // 2 < HEADS:
-                nm((t - 5) // 2)
+        for t in range(-5, NPAIR + 5):
+            if t % 2 == 0 and 0 <= (t - 6) // 2 < HEADS:
+                nm((t - 6) // 2)
             if 0 <= t - 3 < NPAIR:
                 qz(t - 3)
+            if t % 2 == 1 and 0 <= (t - 1) // 2 < HEADS:
+                vprep((t - 1) // 2)
             if t % 2 == 0 and 0 <= (t - 2) // 2 < HEADS:
                 vquant((t - 2) // 2)
+            if 0 <= t - 1 < NPAIR:
+                te(t - 1)
+            k = t + 5
+            if 0 <= k < 2 * HEADS:
+                t1_pe(k // 2, k % 2)
+            if 0 <= t - 4 < NPAIR:
+                mx(t - 4)
             if 0 <= t + 3 < NPAIR:
                 sc(t + 3)
             if 0 <= t + 2 < NPAIR:
                 pre(t + 2)
-            if 0 <= t - 3 < NPAIR:
-                mx(t - 3)
-            if t < NPAIR:
-                filler(FILL)
-            if 0 <= t - 1 < NPAIR:
-                te(t - 1)
-            th, ts = ((t + 5) // 2, 0) if t % 2 == 1 else ((t + 4) // 2, 1)
-            do_t1 = 0 <= th < HEADS
-            if do_t1:
-                t1_pe(th, ts)
             if 0 <= t < NPAIR:
                 ex(t)
             if 0 <= t - 1 < NPAIR:
                 ev(t - 1)
-            if do_t1:
-                t1_ev(th, ts)
+            if 0 <= k < 2 * HEADS:
+                t1_ev(k // 2, k % 2)
             if 0 <= t - 2 < NPAIR:
                 rg(t - 2)
-            if t % 2 == 0 and 0 <= t // 2 < HEADS:
-                vprep(t // 2)

@@ -23,6 +23,9 @@ NPAIR = 2 * HEADS
 C = 1.0 / math.sqrt(128.0)
 FLOPS = 4 * HEADS * T * (2 * KS) * D
 PIN = True
+FILL = 1
+WARM = 4
+PRO = 2
 CHUNKS = ((0, 1), (1, 2), (2, 4), (4, 8), (8, 16))
 
 
@@ -47,6 +50,9 @@ def tile_l1regressionmoeactionhead_pb_kernel(tc, q_a, q_t, k_a, k_t, v_a, v_t, g
         vcodes = res.tile([P, HEADS * D], U32, align_bytes=64)
         vscl = res.tile([P, HEADS * D], U8, align_bytes=64)
         ident = res.tile([P, P], BF16)
+        zc = res.tile([P, 512], U32, align_bytes=64)
+        zs = res.tile([P, 512], U8, align_bytes=64)
+        zb = res.tile([P, 2048], BF16, align_bytes=64)
         eg = res.tile([P, 1], F32)
         ratio = res.tile([P, 1], F32)
         cr = res.tile([P, 1], F32)
@@ -73,6 +79,17 @@ def tile_l1regressionmoeactionhead_pb_kernel(tc, q_a, q_t, k_a, k_t, v_a, v_t, g
             nc.sync.dma_start(out=v_s[:, 1, 2 * h0:2 * h1, :], in_=vt_v[:, 2 * h0:2 * h1, :])
 
         make_identity(nc, ident[:])
+        nc.vector.memset(zb[:].bitcast(I32), 0)
+        nc.vector.quantize_mx(out=zc[:].bitcast(FP8X4), scales=zs[:], in_=zb[:])
+
+        def filler(bank, n):
+            for i in range(n):
+                nc.tensor.matmul_mx(out=bank[:], lhsT=zc[:, 0:P].bitcast(FP8X4), lhsT_scale=zs[:, 0:P],
+                                    rhs=zc[:].bitcast(FP8X4), rhs_scale=zs[:], start=True, stop=True)
+
+        warm = ps_o.tile([P, 512], F32, name="o")
+        filler(warm, WARM)
+
         nc.scalar.activation(out=eg[:], in_=g_sb[:], func=ACT.Exp, scale=-1.0)
         nc.vector.tensor_scalar_add(out=eg[:], in0=eg[:], scalar1=1.0)
         nc.vector.reciprocal(out=ratio[:], in_=eg[:])
@@ -113,6 +130,7 @@ def tile_l1regressionmoeactionhead_pb_kernel(tc, q_a, q_t, k_a, k_t, v_a, v_t, g
             for jj in range(2):
                 j = 2 * (s % 2) + jj
                 sb = ps_s.tile([P, 512], F32, name="sb")
+                filler(sb, FILL)
                 nc.tensor.matmul(out=sb[:, 0:256], lhsT=aT[:, j * P:(j + 1) * P], rhs=aT[:, 512:768], start=True, stop=True)
                 nc.tensor.matmul(out=sb[:, 256:512], lhsT=tT[:, j * P:(j + 1) * P], rhs=tT[:, 512:768], start=True, stop=True)
                 st[("sb", s, jj)] = sb
@@ -224,6 +242,8 @@ def tile_l1regressionmoeactionhead_pb_kernel(tc, q_a, q_t, k_a, k_t, v_a, v_t, g
             k = t + 5
             if 0 <= k < 2 * HEADS:
                 t1_pe(k // 2, k % 2)
+            if t < 0:
+                filler(warm, PRO)
             if 0 <= t - 4 < NPAIR:
                 mx(t - 4)
             if 0 <= t + 3 < NPAIR:

@@ -23,9 +23,6 @@ NPAIR = 2 * HEADS
 C = 1.0 / math.sqrt(128.0)
 FLOPS = 4 * HEADS * T * (2 * KS) * D
 PIN = True
-FILL = 1
-WARM = 4
-PRO = 2
 CHUNKS = ((0, 1), (1, 2), (2, 4), (4, 8), (8, 16))
 
 
@@ -36,10 +33,9 @@ def tile_l1regressionmoeactionhead_pb_kernel(tc, q_a, q_t, k_a, k_t, v_a, v_t, g
             ctx.enter_context(tc.manual_schedule())
         res = ctx.enter_context(tc.tile_pool(name="res", bufs=1))
         wk = ctx.enter_context(tc.tile_pool(name="wk", bufs=3))
-        ps_s = ctx.enter_context(tc.psum_pool(name="ps_s", bufs=4))
-        ps_t1 = ctx.enter_context(tc.psum_pool(name="ps_t1", bufs=1))
-        ps_t2 = ctx.enter_context(tc.psum_pool(name="ps_t2", bufs=2))
-        ps_o = ctx.enter_context(tc.psum_pool(name="ps_o", bufs=1))
+        ps_s = ctx.enter_context(tc.psum_pool(name="ps_s", bufs=3))
+        ps_tt = ctx.enter_context(tc.psum_pool(name="ps_tt", bufs=3))
+        ps_o = ctx.enter_context(tc.psum_pool(name="ps_o", bufs=2))
 
         g_sb = res.tile([P, 1], BF16)
         qa_sb = res.tile([P, HEADS * 512], BF16)
@@ -50,9 +46,6 @@ def tile_l1regressionmoeactionhead_pb_kernel(tc, q_a, q_t, k_a, k_t, v_a, v_t, g
         vcodes = res.tile([P, HEADS * D], U32, align_bytes=64)
         vscl = res.tile([P, HEADS * D], U8, align_bytes=64)
         ident = res.tile([P, P], BF16)
-        zc = res.tile([P, 512], U32, align_bytes=64)
-        zs = res.tile([P, 512], U8, align_bytes=64)
-        zb = res.tile([P, 2048], BF16, align_bytes=64)
         eg = res.tile([P, 1], F32)
         ratio = res.tile([P, 1], F32)
         cr = res.tile([P, 1], F32)
@@ -79,17 +72,6 @@ def tile_l1regressionmoeactionhead_pb_kernel(tc, q_a, q_t, k_a, k_t, v_a, v_t, g
             nc.sync.dma_start(out=v_s[:, 1, 2 * h0:2 * h1, :], in_=vt_v[:, 2 * h0:2 * h1, :])
 
         make_identity(nc, ident[:])
-        nc.vector.memset(zb[:].bitcast(I32), 0)
-        nc.vector.quantize_mx(out=zc[:].bitcast(FP8X4), scales=zs[:], in_=zb[:])
-
-        def filler(bank, n):
-            for i in range(n):
-                nc.tensor.matmul_mx(out=bank[:], lhsT=zc[:, 0:P].bitcast(FP8X4), lhsT_scale=zs[:, 0:P],
-                                    rhs=zc[:].bitcast(FP8X4), rhs_scale=zs[:], start=True, stop=True)
-
-        warm = ps_o.tile([P, 512], F32, name="o")
-        filler(warm, WARM)
-
         nc.scalar.activation(out=eg[:], in_=g_sb[:], func=ACT.Exp, scale=-1.0)
         nc.vector.tensor_scalar_add(out=eg[:], in0=eg[:], scalar1=1.0)
         nc.vector.reciprocal(out=ratio[:], in_=eg[:])
@@ -99,7 +81,7 @@ def tile_l1regressionmoeactionhead_pb_kernel(tc, q_a, q_t, k_a, k_t, v_a, v_t, g
 
         def t1_pe(h, s):
             q_sb, k_sb = (qa_sb, ka_sb) if s == 0 else (qt_sb, kt_sb)
-            t1 = ps_t1.tile([P, 768], BF16, name="t1")
+            t1 = ps_tt.tile([P, 1024], BF16, name="tt")
             for j in range(4):
                 nc.tensor.transpose(t1[:, j * P:(j + 1) * P], q_sb[:, h * 512 + j * P:h * 512 + (j + 1) * P], ident[:])
             for j in range(2):
@@ -108,12 +90,13 @@ def tile_l1regressionmoeactionhead_pb_kernel(tc, q_a, q_t, k_a, k_t, v_a, v_t, g
 
         def t1_ev(h, s):
             xT = wk.tile([P, 768], BF16, name="xT%d" % s, bufs=2)
-            nc.scalar.copy(out=xT[:], in_=st[("t1", h, s)][:])
+            nc.vector.tensor_copy(out=xT[:], in_=st[("t1", h, s)][:, 0:768])
             st[("xT", h, s)] = xT
 
         def vprep(h):
             vg = wk.tile([P, 512], BF16, name="vg", align_bytes=64)
-            nc.vector.tensor_copy(out=vg[:].rearrange("p (d u t) -> p d u t", u=2, t=2), in_=v_r[:, h])
+            nc.gpsimd.tensor_scalar(out=vg[:].rearrange("p (d u t) -> p d u t", u=2, t=2), in0=v_r[:, h],
+                                    scalar1=1.0, scalar2=0.0, op0=ALU.mult, op1=ALU.add)
             st[("vg", h)] = vg
 
         def vquant(h):
@@ -123,17 +106,15 @@ def tile_l1regressionmoeactionhead_pb_kernel(tc, q_a, q_t, k_a, k_t, v_a, v_t, g
                 in_=st[("vg", h)][:],
             )
 
-        def sc(s):
+        def sc(s, jj):
             h = s // 2
             aT = st[("xT", h, 0)]
             tT = st[("xT", h, 1)]
-            for jj in range(2):
-                j = 2 * (s % 2) + jj
-                sb = ps_s.tile([P, 512], F32, name="sb")
-                filler(sb, FILL)
-                nc.tensor.matmul(out=sb[:, 0:256], lhsT=aT[:, j * P:(j + 1) * P], rhs=aT[:, 512:768], start=True, stop=True)
-                nc.tensor.matmul(out=sb[:, 256:512], lhsT=tT[:, j * P:(j + 1) * P], rhs=tT[:, 512:768], start=True, stop=True)
-                st[("sb", s, jj)] = sb
+            j = 2 * (s % 2) + jj
+            sb = ps_s.tile([P, 512], F32, name="sb")
+            nc.tensor.matmul(out=sb[:, 0:256], lhsT=aT[:, j * P:(j + 1) * P], rhs=aT[:, 512:768], start=True, stop=True)
+            nc.tensor.matmul(out=sb[:, 256:512], lhsT=tT[:, j * P:(j + 1) * P], rhs=tT[:, 512:768], start=True, stop=True)
+            st[("sb", s, jj)] = sb
 
         def pre(s):
             mxp = wk.tile([P, 4], F32, name="mxp", bufs=8)
@@ -152,7 +133,7 @@ def tile_l1regressionmoeactionhead_pb_kernel(tc, q_a, q_t, k_a, k_t, v_a, v_t, g
         def ex(s):
             h = s // 2
             if s % 2 == 0:
-                rs = wk.tile([P, 4], F32, name="rs", bufs=6)
+                rs = wk.tile([P, 4], F32, name="rs", bufs=7)
                 st[("rs", h)] = rs
             rs = st[("rs", h)]
             nb = st[("nb", s)]
@@ -165,19 +146,22 @@ def tile_l1regressionmoeactionhead_pb_kernel(tc, q_a, q_t, k_a, k_t, v_a, v_t, g
 
         def te(s):
             e = st[("e", s)]
-            t2 = ps_t2.tile([P, 1024], BF16, name="t2")
+            t2 = ps_tt.tile([P, 1024], BF16, name="tt")
             for i in range(8):
                 nc.tensor.transpose(t2[:, i * P:(i + 1) * P], e[:, i * P:(i + 1) * P], ident[:])
             st[("t2", s)] = t2
 
-        def ev(s):
-            t2 = st[("t2", s)]
+        def ev_v(s):
             et = wk.tile([P, 512], BF16, name="et", bufs=4)
-            gr = wk.tile([P, 1024], BF16, name="gr", align_bytes=64, bufs=6)
-            nc.scalar.copy(out=et[:], in_=t2[:, 0:512])
-            nc.scalar.copy(out=gr[:, 512:1024].rearrange("p (q t) -> p q t", t=4),
-                           in_=t2[:, 512:1024].rearrange("p (t q) -> p q t", t=4))
+            nc.vector.tensor_copy(out=et[:], in_=st[("t2", s)][:, 0:512])
             st[("et", s)] = et
+
+        def ev_s(s):
+            t2 = st[("t2", s)]
+            gr = wk.tile([P, 1024], BF16, name="gr", align_bytes=64, bufs=7)
+            lo = 512 if s % 2 == 0 else 0
+            nc.scalar.copy(out=gr[:, lo:1024].rearrange("p (j q t) -> p j q t", q=P, t=4),
+                           in_=t2[:, lo:1024].rearrange("p (j t q) -> p j q t", q=P, t=4))
             st[("gr", s)] = gr
 
         def rg(s):
@@ -188,8 +172,8 @@ def tile_l1regressionmoeactionhead_pb_kernel(tc, q_a, q_t, k_a, k_t, v_a, v_t, g
             )
 
         def qz(s):
-            codes = wk.tile([P, 256], U32, name="codes", align_bytes=64, bufs=5)
-            scl = wk.tile([P, 256], U8, name="scl", align_bytes=64, bufs=5)
+            codes = wk.tile([P, 256], U32, name="codes", align_bytes=64, bufs=6)
+            scl = wk.tile([P, 256], U8, name="scl", align_bytes=64, bufs=6)
             nc.vector.quantize_mx(out=codes[:].bitcast(FP8X4), scales=scl[:], in_=st[("gr", s)][:])
             st[("cd", s)] = (codes, scl)
 
@@ -211,50 +195,53 @@ def tile_l1regressionmoeactionhead_pb_kernel(tc, q_a, q_t, k_a, k_t, v_a, v_t, g
                     start=True, stop=True,
                 )
 
+        def recip(h):
+            rinv = wk.tile([P, 4], F32, name="rinv", bufs=4)
+            nc.vector.reciprocal(out=rinv[:], in_=st[("rs", h)][:])
+            st[("rinv", h)] = rinv
+
         def nm(h):
-            rs = st[("rs", h)]
-            rinv = wk.tile([P, 4], F32, name="rinv")
+            rinv = st[("rinv", h)]
+            o = st[("o", h)]
             osb = wk.tile([P, 512], F32, name="osb")
-            nc.vector.reciprocal(out=rinv[:], in_=rs[:])
-            nc.vector.tensor_tensor(
-                out=osb[:].rearrange("p (j d) -> p j d", d=D),
-                in0=st[("o", h)][:].rearrange("p (j d) -> p j d", d=D),
-                in1=rinv[:].unsqueeze(2).to_broadcast([P, 4, D]),
-                op=ALU.mult,
-            )
+            for j in range(4):
+                nc.scalar.activation(out=osb[:, j * D:(j + 1) * D], in_=o[:, j * D:(j + 1) * D], func=ACT.Copy, scale=rinv[:, j:j + 1])
             n, hh = divmod(h, 8)
             nc.sync.dma_start(
                 out=out[n].rearrange("(p j) c -> p j c", j=4)[:, :, hh * D:(hh + 1) * D],
                 in_=osb[:].rearrange("p (j d) -> p j d", d=D),
             )
 
-        for t in range(-5, NPAIR + 5):
-            if t % 2 == 0 and 0 <= (t - 6) // 2 < HEADS:
-                nm((t - 6) // 2)
-            if 0 <= t - 3 < NPAIR:
-                qz(t - 3)
-            if t % 2 == 1 and 0 <= (t - 1) // 2 < HEADS:
-                vprep((t - 1) // 2)
+        for t in range(-6, NPAIR + 6):
+            if t % 2 == 1 and 0 <= (t - 5) // 2 < HEADS:
+                recip((t - 5) // 2)
+            if 0 <= t - 4 < NPAIR:
+                qz(t - 4)
             if t % 2 == 0 and 0 <= (t - 2) // 2 < HEADS:
                 vquant((t - 2) // 2)
+            if 0 <= t + 2 < NPAIR:
+                sc(t + 2, 1)
             if 0 <= t - 1 < NPAIR:
                 te(t - 1)
-            k = t + 5
-            if 0 <= k < 2 * HEADS:
-                t1_pe(k // 2, k % 2)
-            if t < 0:
-                filler(warm, PRO)
-            if 0 <= t - 4 < NPAIR:
-                mx(t - 4)
+            if 0 <= t + 6 < 2 * HEADS:
+                t1_pe((t + 6) // 2, (t + 6) % 2)
             if 0 <= t + 3 < NPAIR:
-                sc(t + 3)
+                sc(t + 3, 0)
+            if 0 <= t - 5 < NPAIR:
+                mx(t - 5)
+            if 0 <= t + 5 < 2 * HEADS:
+                t1_ev((t + 5) // 2, (t + 5) % 2)
+            if 0 <= t - 1 < NPAIR and (t - 1) % 2 == 0:
+                ev_v(t - 1)
             if 0 <= t + 2 < NPAIR:
                 pre(t + 2)
             if 0 <= t < NPAIR:
                 ex(t)
             if 0 <= t - 1 < NPAIR:
-                ev(t - 1)
-            if 0 <= k < 2 * HEADS:
-                t1_ev(k // 2, k % 2)
-            if 0 <= t - 2 < NPAIR:
+                ev_s(t - 1)
+            if t % 2 == 1 and 0 <= (t - 7) // 2 < HEADS:
+                nm((t - 7) // 2)
+            if 0 <= t - 2 < NPAIR and (t - 2) % 2 == 0:
                 rg(t - 2)
+            if t % 2 == 1 and 0 <= (t - 1) // 2 < HEADS:
+                vprep((t - 1) // 2)

@@ -23,7 +23,7 @@ NPAIR = 2 * HEADS
 C = 1.0 / math.sqrt(128.0)
 FLOPS = 4 * HEADS * T * (2 * KS) * D
 PIN = True
-CHUNKS = ((0, 1), (1, 2), (2, 4), (4, 8), (8, 16))
+CHUNKS = ((0, 1), (1, 2), (2, 4), (4, 8), (8, 12), (12, 16))
 
 
 def tile_l1regressionmoeactionhead_pb_kernel(tc, q_a, q_t, k_a, k_t, v_a, v_t, gating_factor, out):
@@ -53,23 +53,23 @@ def tile_l1regressionmoeactionhead_pb_kernel(tc, q_a, q_t, k_a, k_t, v_a, v_t, g
         nc.sync.dma_start(out=g_sb[:], in_=gating_factor.partition_broadcast(P))
         qa_v = q_a.rearrange("b h (p j) d -> p (b h) (j d)", j=4)
         qt_v = q_t.rearrange("b h (p j) d -> p (b h) (j d)", j=4)
-        ka_v = k_a.rearrange("b h (j p) d -> p (b h j) d", p=P)
-        kt_v = k_t.rearrange("b h (j p) d -> p (b h j) d", p=P)
-        va_v = v_a.rearrange("b h (t p) d -> p (b h t) d", p=P)
-        vt_v = v_t.rearrange("b h (t p) d -> p (b h t) d", p=P)
+        ka_v = k_a.rearrange("b h (p j) d -> p (b h) (j d)", j=2)
+        kt_v = k_t.rearrange("b h (p j) d -> p (b h) (j d)", j=2)
+        va_v = v_a.rearrange("b h (p t) d -> p (b h) (t d)", t=2)
+        vt_v = v_t.rearrange("b h (p t) d -> p (b h) (t d)", t=2)
         qa_s = qa_sb[:].rearrange("p (h x) -> p h x", x=512)
         qt_s = qt_sb[:].rearrange("p (h x) -> p h x", x=512)
-        ka_s = ka_sb[:].rearrange("p (g d) -> p g d", d=D)
-        kt_s = kt_sb[:].rearrange("p (g d) -> p g d", d=D)
-        v_s = v_sb[:].rearrange("p (u g d) -> p u g d", u=2, d=D)
+        ka_s = ka_sb[:].rearrange("p (h x) -> p h x", x=256)
+        kt_s = kt_sb[:].rearrange("p (h x) -> p h x", x=256)
+        v_s = v_sb[:].rearrange("p (u h x) -> p u h x", u=2, x=256)
         v_r = v_sb[:].rearrange("p (u h t d) -> p h d u t", u=2, t=2, d=D)
         for h0, h1 in CHUNKS:
-            nc.sync.dma_start(out=ka_s[:, 2 * h0:2 * h1, :], in_=ka_v[:, 2 * h0:2 * h1, :])
+            nc.sync.dma_start(out=ka_s[:, h0:h1, :], in_=ka_v[:, h0:h1, :])
             nc.sync.dma_start(out=qa_s[:, h0:h1, :], in_=qa_v[:, h0:h1, :])
-            nc.sync.dma_start(out=kt_s[:, 2 * h0:2 * h1, :], in_=kt_v[:, 2 * h0:2 * h1, :])
+            nc.sync.dma_start(out=kt_s[:, h0:h1, :], in_=kt_v[:, h0:h1, :])
             nc.sync.dma_start(out=qt_s[:, h0:h1, :], in_=qt_v[:, h0:h1, :])
-            nc.sync.dma_start(out=v_s[:, 0, 2 * h0:2 * h1, :], in_=va_v[:, 2 * h0:2 * h1, :])
-            nc.sync.dma_start(out=v_s[:, 1, 2 * h0:2 * h1, :], in_=vt_v[:, 2 * h0:2 * h1, :])
+            nc.sync.dma_start(out=v_s[:, 0, h0:h1, :], in_=va_v[:, h0:h1, :])
+            nc.sync.dma_start(out=v_s[:, 1, h0:h1, :], in_=vt_v[:, h0:h1, :])
 
         make_identity(nc, ident[:])
         nc.scalar.activation(out=eg[:], in_=g_sb[:], func=ACT.Exp, scale=-1.0)

@@ -23,7 +23,10 @@ NPAIR = 2 * HEADS
 C = 1.0 / math.sqrt(128.0)
 FLOPS = 4 * HEADS * T * (2 * KS) * D
 PIN = True
-CHUNKS = ((0, 1), (1, 2), (2, 4), (4, 8), (8, 12), (12, 16))
+T1S = 7
+NMV = 3
+EVV = 4
+CHUNKS = ((2, 4), (4, 8), (8, 12), (12, 16))
 
 
 def tile_l1regressionmoeactionhead_pb_kernel(tc, q_a, q_t, k_a, k_t, v_a, v_t, gating_factor, out):
@@ -34,8 +37,8 @@ def tile_l1regressionmoeactionhead_pb_kernel(tc, q_a, q_t, k_a, k_t, v_a, v_t, g
         res = ctx.enter_context(tc.tile_pool(name="res", bufs=1))
         wk = ctx.enter_context(tc.tile_pool(name="wk", bufs=3))
         ps_s = ctx.enter_context(tc.psum_pool(name="ps_s", bufs=3))
-        ps_tt = ctx.enter_context(tc.psum_pool(name="ps_tt", bufs=3))
-        ps_o = ctx.enter_context(tc.psum_pool(name="ps_o", bufs=2))
+        ps_tt = ctx.enter_context(tc.psum_pool(name="ps_tt", bufs=4))
+        ps_o = ctx.enter_context(tc.psum_pool(name="ps_o", bufs=1))
 
         g_sb = res.tile([P, 1], BF16)
         qa_sb = res.tile([P, HEADS * 512], BF16)
@@ -63,13 +66,22 @@ def tile_l1regressionmoeactionhead_pb_kernel(tc, q_a, q_t, k_a, k_t, v_a, v_t, g
         kt_s = kt_sb[:].rearrange("p (h x) -> p h x", x=256)
         v_s = v_sb[:].rearrange("p (u h x) -> p u h x", u=2, x=256)
         v_r = v_sb[:].rearrange("p (u h t d) -> p h d u t", u=2, t=2, d=D)
-        for h0, h1 in CHUNKS:
+        def load_kq(h0, h1):
             nc.sync.dma_start(out=ka_s[:, h0:h1, :], in_=ka_v[:, h0:h1, :])
             nc.sync.dma_start(out=qa_s[:, h0:h1, :], in_=qa_v[:, h0:h1, :])
             nc.sync.dma_start(out=kt_s[:, h0:h1, :], in_=kt_v[:, h0:h1, :])
             nc.sync.dma_start(out=qt_s[:, h0:h1, :], in_=qt_v[:, h0:h1, :])
+
+        def load_v(h0, h1):
             nc.sync.dma_start(out=v_s[:, 0, h0:h1, :], in_=va_v[:, h0:h1, :])
             nc.sync.dma_start(out=v_s[:, 1, h0:h1, :], in_=vt_v[:, h0:h1, :])
+
+        load_kq(0, 1)
+        load_kq(1, 2)
+        load_v(0, 2)
+        for h0, h1 in CHUNKS:
+            load_kq(h0, h1)
+            load_v(h0, h1)
 
         make_identity(nc, ident[:])
         nc.scalar.activation(out=eg[:], in_=g_sb[:], func=ACT.Exp, scale=-1.0)
@@ -90,20 +102,26 @@ def tile_l1regressionmoeactionhead_pb_kernel(tc, q_a, q_t, k_a, k_t, v_a, v_t, g
 
         def t1_ev(h, s):
             xT = wk.tile([P, 768], BF16, name="xT%d" % s, bufs=2)
-            nc.vector.tensor_copy(out=xT[:], in_=st[("t1", h, s)][:, 0:768])
+            if 1 <= 2 * h + s < T1S or (2 * h + s) % 4 == 0 and h > 0:
+                nc.scalar.copy(out=xT[:], in_=st[("t1", h, s)][:, 0:768])
+            else:
+                nc.vector.tensor_copy(out=xT[:], in_=st[("t1", h, s)][:, 0:768])
             st[("xT", h, s)] = xT
 
         def vprep(h):
-            vg = wk.tile([P, 512], BF16, name="vg", align_bytes=64)
-            nc.gpsimd.tensor_scalar(out=vg[:].rearrange("p (d u t) -> p d u t", u=2, t=2), in0=v_r[:, h],
+            if h % 4 == 0:
+                vg = wk.tile([P, 2048], BF16, name="vg", align_bytes=64, bufs=2)
+                st[("vg", h // 4)] = vg
+            vg = st[("vg", h // 4)]
+            lo = (h % 4) * 512
+            nc.gpsimd.tensor_scalar(out=vg[:, lo:lo + 512].rearrange("p (d u t) -> p d u t", u=2, t=2), in0=v_r[:, h],
                                     scalar1=1.0, scalar2=0.0, op0=ALU.mult, op1=ALU.add)
-            st[("vg", h)] = vg
 
-        def vquant(h):
+        def vquant(g):
             nc.vector.quantize_mx(
-                out=vcodes[:, h * D:(h + 1) * D].bitcast(FP8X4),
-                scales=vscl[:, h * D:(h + 1) * D],
-                in_=st[("vg", h)][:],
+                out=vcodes[:, g * 512:(g + 1) * 512].bitcast(FP8X4),
+                scales=vscl[:, g * 512:(g + 1) * 512],
+                in_=st[("vg", g)][:],
             )
 
         def sc(s, jj):
@@ -133,11 +151,11 @@ def tile_l1regressionmoeactionhead_pb_kernel(tc, q_a, q_t, k_a, k_t, v_a, v_t, g
         def ex(s):
             h = s // 2
             if s % 2 == 0:
-                rs = wk.tile([P, 4], F32, name="rs", bufs=7)
+                rs = wk.tile([P, 4], F32, name="rs", bufs=8)
                 st[("rs", h)] = rs
             rs = st[("rs", h)]
             nb = st[("nb", s)]
-            e = wk.tile([P, 1024], BF16, name="e", bufs=4)
+            e = wk.tile([P, 1024], BF16, name="e", bufs=5)
             for jj in range(2):
                 j = 2 * (s % 2) + jj
                 nc.scalar.activation(out=e[:, jj * 512:(jj + 1) * 512], in_=st[("x", s, jj)][:], func=ACT.Exp,
@@ -158,38 +176,41 @@ def tile_l1regressionmoeactionhead_pb_kernel(tc, q_a, q_t, k_a, k_t, v_a, v_t, g
 
         def ev_s(s):
             t2 = st[("t2", s)]
-            gr = wk.tile([P, 1024], BF16, name="gr", align_bytes=64, bufs=7)
-            lo = 512 if s % 2 == 0 else 0
-            nc.scalar.copy(out=gr[:, lo:1024].rearrange("p (j q t) -> p j q t", q=P, t=4),
+            if s % 2 == 0:
+                gr = wk.tile([P, 2048], BF16, name="gr", align_bytes=64, bufs=4)
+                st[("gr", s // 2)] = gr
+            gr = st[("gr", s // 2)]
+            b0 = (s % 2) * 1024
+            lo = 512 if (s % 2 == 0 or s >= NPAIR - EVV) else 0
+            if s >= NPAIR - EVV:
+                nc.vector.tensor_copy(out=gr[:, b0:b0 + 512].rearrange("p (q t) -> p q t", t=4),
+                                      in_=t2[:, 0:512].rearrange("p (t q) -> p q t", t=4))
+            nc.scalar.copy(out=gr[:, b0 + lo:b0 + 1024].rearrange("p (j q t) -> p j q t", q=P, t=4),
                            in_=t2[:, lo:1024].rearrange("p (j t q) -> p j q t", q=P, t=4))
-            st[("gr", s)] = gr
 
         def rg(s):
+            b0 = (s % 2) * 1024
             nc.gpsimd.tensor_scalar(
-                out=st[("gr", s)][:, 0:512].rearrange("p (q t) -> p q t", t=4),
+                out=st[("gr", s // 2)][:, b0:b0 + 512].rearrange("p (q t) -> p q t", t=4),
                 in0=st[("et", s)][:].rearrange("p (t q) -> p q t", t=4),
                 scalar1=1.0, scalar2=0.0, op0=ALU.mult, op1=ALU.add,
             )
 
-        def qz(s):
-            codes = wk.tile([P, 256], U32, name="codes", align_bytes=64, bufs=6)
-            scl = wk.tile([P, 256], U8, name="scl", align_bytes=64, bufs=6)
-            nc.vector.quantize_mx(out=codes[:].bitcast(FP8X4), scales=scl[:], in_=st[("gr", s)][:])
-            st[("cd", s)] = (codes, scl)
+        def qz(h):
+            codes = wk.tile([P, 512], U32, name="codes", align_bytes=64, bufs=3)
+            scl = wk.tile([P, 512], U8, name="scl", align_bytes=64, bufs=3)
+            nc.vector.quantize_mx(out=codes[:].bitcast(FP8X4), scales=scl[:], in_=st[("gr", h)][:])
+            st[("cd", h)] = (codes, scl)
 
-        def mx(s):
-            h = s // 2
-            if s % 2 == 0:
-                o = ps_o.tile([P, 512], F32, name="o")
-                st[("o", h)] = o
-            o = st[("o", h)]
-            codes, scl = st[("cd", s)]
-            for jj in range(2):
-                j = 2 * (s % 2) + jj
+        def mx(h):
+            o = ps_o.tile([P, 512], F32, name="o")
+            st[("o", h)] = o
+            codes, scl = st[("cd", h)]
+            for j in range(4):
                 nc.tensor.matmul_mx(
                     out=o[:, j * D:(j + 1) * D],
-                    lhsT=codes[:, jj * P:(jj + 1) * P].bitcast(FP8X4),
-                    lhsT_scale=scl[:, jj * P:(jj + 1) * P],
+                    lhsT=codes[:, j * P:(j + 1) * P].bitcast(FP8X4),
+                    lhsT_scale=scl[:, j * P:(j + 1) * P],
                     rhs=vcodes[:, h * D:(h + 1) * D].bitcast(FP8X4),
                     rhs_scale=vscl[:, h * D:(h + 1) * D],
                     start=True, stop=True,
@@ -204,7 +225,10 @@ def tile_l1regressionmoeactionhead_pb_kernel(tc, q_a, q_t, k_a, k_t, v_a, v_t, g
             rinv = st[("rinv", h)]
             o = st[("o", h)]
             osb = wk.tile([P, 512], F32, name="osb")
-            for j in range(4):
+            if h >= HEADS - NMV:
+                nc.vector.tensor_tensor(out=osb[:].rearrange("p (j d) -> p j d", d=D), in0=o[:].rearrange("p (j d) -> p j d", d=D),
+                                        in1=rinv[:].unsqueeze(2).to_broadcast([P, 4, D]), op=ALU.mult)
+            for j in range(4 if h < HEADS - NMV else 0):
                 nc.scalar.activation(out=osb[:, j * D:(j + 1) * D], in_=o[:, j * D:(j + 1) * D], func=ACT.Copy, scale=rinv[:, j:j + 1])
             n, hh = divmod(h, 8)
             nc.sync.dma_start(
@@ -212,36 +236,38 @@ def tile_l1regressionmoeactionhead_pb_kernel(tc, q_a, q_t, k_a, k_t, v_a, v_t, g
                 in_=osb[:].rearrange("p (j d) -> p j d", d=D),
             )
 
-        for t in range(-6, NPAIR + 6):
+        for t in range(-6, NPAIR + 7):
             if t % 2 == 1 and 0 <= (t - 5) // 2 < HEADS:
                 recip((t - 5) // 2)
-            if 0 <= t - 4 < NPAIR:
-                qz(t - 4)
-            if t % 2 == 0 and 0 <= (t - 2) // 2 < HEADS:
-                vquant((t - 2) // 2)
+            if t % 2 == 0 and 0 <= (t - 6) // 2 < HEADS:
+                qz((t - 6) // 2)
+            if (t - 6) % 4 == 0 and 0 <= (t - 6) // 4 < HEADS // 4:
+                vquant((t - 6) // 4)
             if 0 <= t + 2 < NPAIR:
                 sc(t + 2, 1)
+            if t < 0 and 0 <= t + 3 < NPAIR:
+                sc(t + 3, 0)
             if 0 <= t - 1 < NPAIR:
                 te(t - 1)
             if 0 <= t + 6 < 2 * HEADS:
                 t1_pe((t + 6) // 2, (t + 6) % 2)
-            if 0 <= t + 3 < NPAIR:
+            if t >= 0 and 0 <= t + 3 < NPAIR:
                 sc(t + 3, 0)
-            if 0 <= t - 5 < NPAIR:
-                mx(t - 5)
+            if t % 2 == 1 and 0 <= (t - 7) // 2 < HEADS:
+                mx((t - 7) // 2)
             if 0 <= t + 5 < 2 * HEADS:
                 t1_ev((t + 5) // 2, (t + 5) % 2)
-            if 0 <= t - 1 < NPAIR and (t - 1) % 2 == 0:
-                ev_v(t - 1)
+            if 0 <= t - 2 < NPAIR - EVV and (t - 2) % 2 == 0:
+                ev_v(t - 2)
             if 0 <= t + 2 < NPAIR:
                 pre(t + 2)
             if 0 <= t < NPAIR:
                 ex(t)
-            if 0 <= t - 1 < NPAIR:
-                ev_s(t - 1)
-            if t % 2 == 1 and 0 <= (t - 7) // 2 < HEADS:
-                nm((t - 7) // 2)
-            if 0 <= t - 2 < NPAIR and (t - 2) % 2 == 0:
-                rg(t - 2)
-            if t % 2 == 1 and 0 <= (t - 1) // 2 < HEADS:
-                vprep((t - 1) // 2)
+            if 0 <= t - 2 < NPAIR:
+                ev_s(t - 2)
+            if t % 2 == 0 and 0 <= (t - 8) // 2 < HEADS:
+                nm((t - 8) // 2)
+            if 0 <= t - 3 < NPAIR - EVV and (t - 3) % 2 == 0:
+                rg(t - 3)
+            if 0 <= t - 1 < HEADS:
+                vprep(t - 1)

import math
from contextlib import ExitStack

import concourse.mybir as mybir
from concourse.masks import make_identity

BF16 = mybir.dt.bfloat16
F32 = mybir.dt.float32
U32 = mybir.dt.uint32
U8 = mybir.dt.uint8
I32 = mybir.dt.int32
FP8X4 = mybir.dt.float8_e4m3fn_x4
ALU = mybir.AluOpType
ACT = mybir.ActivationFunctionType
AX = mybir.AxisListType

P = 128
HEADS = 16
T = 512
KS = 256
D = 128
NPAIR = 2 * HEADS
C = 1.0 / math.sqrt(128.0)
FLOPS = 4 * HEADS * T * (2 * KS) * D
PIN = True
T1S = 7
NMV = 3
EVV = 4
CHUNKS = ((2, 4), (4, 8), (8, 12), (12, 16))


def tile_l1regressionmoeactionhead_pb_kernel(tc, q_a, q_t, k_a, k_t, v_a, v_t, gating_factor, out):
    nc = tc.nc
    with ExitStack() as ctx:
        if PIN:
            ctx.enter_context(tc.manual_schedule())
        res = ctx.enter_context(tc.tile_pool(name="res", bufs=1))
        wk = ctx.enter_context(tc.tile_pool(name="wk", bufs=3))
        ps_s = ctx.enter_context(tc.psum_pool(name="ps_s", bufs=3))
        ps_tt = ctx.enter_context(tc.psum_pool(name="ps_tt", bufs=4))
        ps_o = ctx.enter_context(tc.psum_pool(name="ps_o", bufs=1))

        g_sb = res.tile([P, 1], BF16)
        qa_sb = res.tile([P, HEADS * 512], BF16)
        qt_sb = res.tile([P, HEADS * 512], BF16)
        ka_sb = res.tile([P, HEADS * 256], BF16)
        kt_sb = res.tile([P, HEADS * 256], BF16)
        v_sb = res.tile([P, HEADS * 512], BF16)
        vcodes = res.tile([P, HEADS * D], U32, align_bytes=64)
        vscl = res.tile([P, HEADS * D], U8, align_bytes=64)
        ident = res.tile([P, P], BF16)
        eg = res.tile([P, 1], F32)
        ratio = res.tile([P, 1], F32)
        cr = res.tile([P, 1], F32)

        nc.sync.dma_start(out=g_sb[:], in_=gating_factor.partition_broadcast(P))
        qa_v = q_a.rearrange("b h (p j) d -> p (b h) (j d)", j=4)
        qt_v = q_t.rearrange("b h (p j) d -> p (b h) (j d)", j=4)
        ka_v = k_a.rearrange("b h (p j) d -> p (b h) (j d)", j=2)
        kt_v = k_t.rearrange("b h (p j) d -> p (b h) (j d)", j=2)
        va_v = v_a.rearrange("b h (p t) d -> p (b h) (t d)", t=2)
        vt_v = v_t.rearrange("b h (p t) d -> p (b h) (t d)", t=2)
        qa_s = qa_sb[:].rearrange("p (h x) -> p h x", x=512)
        qt_s = qt_sb[:].rearrange("p (h x) -> p h x", x=512)
        ka_s = ka_sb[:].rearrange("p (h x) -> p h x", x=256)
        kt_s = kt_sb[:].rearrange("p (h x) -> p h x", x=256)
        v_s = v_sb[:].rearrange("p (u h x) -> p u h x", u=2, x=256)
        v_r = v_sb[:].rearrange("p (u h t d) -> p h d u t", u=2, t=2, d=D)
        def load_kq(h0, h1):
            nc.sync.dma_start(out=ka_s[:, h0:h1, :], in_=ka_v[:, h0:h1, :])
            nc.sync.dma_start(out=qa_s[:, h0:h1, :], in_=qa_v[:, h0:h1, :])
            nc.sync.dma_start(out=kt_s[:, h0:h1, :], in_=kt_v[:, h0:h1, :])
            nc.sync.dma_start(out=qt_s[:, h0:h1, :], in_=qt_v[:, h0:h1, :])

        def load_v(h0, h1):
            nc.sync.dma_start(out=v_s[:, 0, h0:h1, :], in_=va_v[:, h0:h1, :])
            nc.sync.dma_start(out=v_s[:, 1, h0:h1, :], in_=vt_v[:, h0:h1, :])

        load_kq(0, 1)
        load_kq(1, 2)
        load_v(0, 2)
        for h0, h1 in CHUNKS:
            load_kq(h0, h1)
            load_v(h0, h1)

        make_identity(nc, ident[:])
        nc.scalar.activation(out=eg[:], in_=g_sb[:], func=ACT.Exp, scale=-1.0)
        nc.vector.tensor_scalar_add(out=eg[:], in0=eg[:], scalar1=1.0)
        nc.vector.reciprocal(out=ratio[:], in_=eg[:])
        nc.vector.tensor_scalar_mul(out=cr[:], in0=ratio[:], scalar1=C)

        st = {}

        def t1_pe(h, s):
            q_sb, k_sb = (qa_sb, ka_sb) if s == 0 else (qt_sb, kt_sb)
            t1 = ps_tt.tile([P, 1024], BF16, name="tt")
            for j in range(4):
                nc.tensor.transpose(t1[:, j * P:(j + 1) * P], q_sb[:, h * 512 + j * P:h * 512 + (j + 1) * P], ident[:])
            for j in range(2):
                nc.tensor.transpose(t1[:, 512 + j * P:512 + (j + 1) * P], k_sb[:, h * 256 + j * P:h * 256 + (j + 1) * P], ident[:])
            st[("t1", h, s)] = t1

        def t1_ev(h, s):
            xT = wk.tile([P, 768], BF16, name="xT%d" % s, bufs=2)
            if 1 <= 2 * h + s < T1S or (2 * h + s) % 4 == 0 and h > 0:
                nc.scalar.copy(out=xT[:], in_=st[("t1", h, s)][:, 0:768])
            else:
                nc.vector.tensor_copy(out=xT[:], in_=st[("t1", h, s)][:, 0:768])
            st[("xT", h, s)] = xT

        def vprep(h):
            if h % 4 == 0:
                vg = wk.tile([P, 2048], BF16, name="vg", align_bytes=64, bufs=2)
                st[("vg", h // 4)] = vg
            vg = st[("vg", h // 4)]
            lo = (h % 4) * 512
            nc.gpsimd.tensor_scalar(out=vg[:, lo:lo + 512].rearrange("p (d u t) -> p d u t", u=2, t=2), in0=v_r[:, h],
                                    scalar1=1.0, scalar2=0.0, op0=ALU.mult, op1=ALU.add)

        def vquant(g):
            nc.vector.quantize_mx(
                out=vcodes[:, g * 512:(g + 1) * 512].bitcast(FP8X4),
                scales=vscl[:, g * 512:(g + 1) * 512],
                in_=st[("vg", g)][:],
            )

        def sc(s, jj):
            h = s // 2
            aT = st[("xT", h, 0)]
            tT = st[("xT", h, 1)]
            j = 2 * (s % 2) + jj
            sb = ps_s.tile([P, 512], F32, name="sb")
            nc.tensor.matmul(out=sb[:, 0:256], lhsT=aT[:, j * P:(j + 1) * P], rhs=aT[:, 512:768], start=True, stop=True)
            nc.tensor.matmul(out=sb[:, 256:512], lhsT=tT[:, j * P:(j + 1) * P], rhs=tT[:, 512:768], start=True, stop=True)
            st[("sb", s, jj)] = sb

        def pre(s):
            mxp = wk.tile([P, 4], F32, name="mxp", bufs=8)
            nb = wk.tile([P, 2], F32, name="nb", bufs=8)
            for jj in range(2):
                sb = st[("sb", s, jj)]
                x = wk.tile([P, 512], F32, name="x", bufs=10)
                nc.vector.tensor_scalar(out=x[:, 0:256], in0=sb[:, 0:256], scalar1=C, scalar2=None,
                                        op0=ALU.mult, op1=ALU.max, accum_out=mxp[:, 2 * jj:2 * jj + 1])
                nc.vector.tensor_scalar(out=x[:, 256:512], in0=sb[:, 256:512], scalar1=cr[:, 0:1], scalar2=None,
                                        op0=ALU.mult, op1=ALU.max, accum_out=mxp[:, 2 * jj + 1:2 * jj + 2])
                st[("x", s, jj)] = x
            nc.vector.tensor_reduce(out=nb[:], in_=mxp[:].rearrange("p (j u) -> p j u", u=2), axis=AX.X, op=ALU.max, negate=True)
            st[("nb", s)] = nb

        def ex(s):
            h = s // 2
            if s % 2 == 0:
                rs = wk.tile([P, 4], F32, name="rs", bufs=8)
                st[("rs", h)] = rs
            rs = st[("rs", h)]
            nb = st[("nb", s)]
            e = wk.tile([P, 1024], BF16, name="e", bufs=5)
            for jj in range(2):
                j = 2 * (s % 2) + jj
                nc.scalar.activation(out=e[:, jj * 512:(jj + 1) * 512], in_=st[("x", s, jj)][:], func=ACT.Exp,
                                     bias=nb[:, jj:jj + 1], scale=1.0, accum_out=rs[:, j:j + 1])
            st[("e", s)] = e

        def te(s):
            e = st[("e", s)]
            t2 = ps_tt.tile([P, 1024], BF16, name="tt")
            for i in range(8):
                nc.tensor.transpose(t2[:, i * P:(i + 1) * P], e[:, i * P:(i + 1) * P], ident[:])
            st[("t2", s)] = t2

        def ev_v(s):
            et = wk.tile([P, 512], BF16, name="et", bufs=4)
            nc.vector.tensor_copy(out=et[:], in_=st[("t2", s)][:, 0:512])
            st[("et", s)] = et

        def ev_s(s):
            t2 = st[("t2", s)]
            if s % 2 == 0:
                gr = wk.tile([P, 2048], BF16, name="gr", align_bytes=64, bufs=4)
                st[("gr", s // 2)] = gr
            gr = st[("gr", s // 2)]
            b0 = (s % 2) * 1024
            lo = 512 if (s % 2 == 0 or s >= NPAIR - EVV) else 0
            if s >= NPAIR - EVV:
                nc.vector.tensor_copy(out=gr[:, b0:b0 + 512].rearrange("p (q t) -> p q t", t=4),
                                      in_=t2[:, 0:512].rearrange("p (t q) -> p q t", t=4))
            nc.scalar.copy(out=gr[:, b0 + lo:b0 + 1024].rearrange("p (j q t) -> p j q t", q=P, t=4),
                           in_=t2[:, lo:1024].rearrange("p (j t q) -> p j q t", q=P, t=4))

        def rg(s):
            b0 = (s % 2) * 1024
            nc.gpsimd.tensor_scalar(
                out=st[("gr", s // 2)][:, b0:b0 + 512].rearrange("p (q t) -> p q t", t=4),
                in0=st[("et", s)][:].rearrange("p (t q) -> p q t", t=4),
                scalar1=1.0, scalar2=0.0, op0=ALU.mult, op1=ALU.add,
            )

        def qz(h):
            codes = wk.tile([P, 512], U32, name="codes", align_bytes=64, bufs=3)
            scl = wk.tile([P, 512], U8, name="scl", align_bytes=64, bufs=3)
            nc.vector.quantize_mx(out=codes[:].bitcast(FP8X4), scales=scl[:], in_=st[("gr", h)][:])
            st[("cd", h)] = (codes, scl)

        def mx(h):
            o = ps_o.tile([P, 512], F32, name="o")
            st[("o", h)] = o
            codes, scl = st[("cd", h)]
            for j in range(4):
                nc.tensor.matmul_mx(
                    out=o[:, j * D:(j + 1) * D],
                    lhsT=codes[:, j * P:(j + 1) * P].bitcast(FP8X4),
                    lhsT_scale=scl[:, j * P:(j + 1) * P],
                    rhs=vcodes[:, h * D:(h + 1) * D].bitcast(FP8X4),
                    rhs_scale=vscl[:, h * D:(h + 1) * D],
                    start=True, stop=True,
                )

        def recip(h):
            rinv = wk.tile([P, 4], F32, name="rinv", bufs=4)
            nc.vector.reciprocal(out=rinv[:], in_=st[("rs", h)][:])
            st[("rinv", h)] = rinv

        def nm(h):
            rinv = st[("rinv", h)]
            o = st[("o", h)]
            osb = wk.tile([P, 512], F32, name="osb")
            if h >= HEADS - NMV:
                nc.vector.tensor_tensor(out=osb[:].rearrange("p (j d) -> p j d", d=D), in0=o[:].rearrange("p (j d) -> p j d", d=D),
                                        in1=rinv[:].unsqueeze(2).to_broadcast([P, 4, D]), op=ALU.mult)
            for j in range(4 if h < HEADS - NMV else 0):
                nc.scalar.activation(out=osb[:, j * D:(j + 1) * D], in_=o[:, j * D:(j + 1) * D], func=ACT.Copy, scale=rinv[:, j:j + 1])
            n, hh = divmod(h, 8)
            nc.sync.dma_start(
                out=out[n].rearrange("(p j) c -> p j c", j=4)[:, :, hh * D:(hh + 1) * D],
                in_=osb[:].rearrange("p (j d) -> p j d", d=D),
            )

        for t in range(-6, NPAIR + 7):
            if t % 2 == 1 and 0 <= (t - 5) // 2 < HEADS:
                recip((t - 5) // 2)
            if t % 2 == 0 and 0 <= (t - 6) // 2 < HEADS:
                qz((t - 6) // 2)
            if (t - 6) % 4 == 0 and 0 <= (t - 6) // 4 < HEADS // 4:
                vquant((t - 6) // 4)
            if 0 <= t + 2 < NPAIR:
                sc(t + 2, 1)
            if t < 0 and 0 <= t + 3 < NPAIR:
                sc(t + 3, 0)
            if 0 <= t - 1 < NPAIR:
                te(t - 1)
            if 0 <= t + 6 < 2 * HEADS:
                t1_pe((t + 6) // 2, (t + 6) % 2)
            if t >= 0 and 0 <= t + 3 < NPAIR:
                sc(t + 3, 0)
            if t % 2 == 1 and 0 <= (t - 7) // 2 < HEADS:
                mx((t - 7) // 2)
            if 0 <= t + 5 < 2 * HEADS:
                t1_ev((t + 5) // 2, (t + 5) % 2)
            if 0 <= t - 2 < NPAIR - EVV and (t - 2) % 2 == 0:
                ev_v(t - 2)
            if 0 <= t + 2 < NPAIR:
                pre(t + 2)
            if 0 <= t < NPAIR:
                ex(t)
            if 0 <= t - 2 < NPAIR:
                ev_s(t - 2)
            if t % 2 == 0 and 0 <= (t - 8) // 2 < HEADS:
                nm((t - 8) // 2)
            if 0 <= t - 3 < NPAIR - EVV and (t - 3) % 2 == 0:
                rg(t - 3)
            if 0 <= t - 1 < HEADS:
                vprep(t - 1)
